import numpy as np
import ml_dtypes


def mxq(x, axis, fmt="e4m3"):
    dtype, down = {"e4m3": (ml_dtypes.float8_e4m3fn, 7), "e5m2": (ml_dtypes.float8_e5m2, 14)}[fmt]
    v = np.moveaxis(np.asarray(x, np.float32).astype(ml_dtypes.bfloat16).astype(np.float64), axis, -1)
    blocks = v.reshape(v.shape[:-1] + (-1, 32))
    amax = np.abs(blocks).max(-1, keepdims=True)
    byte = np.maximum(np.where(amax > 0, np.frexp(amax)[1] - 1 + 127, 0) - down, 1)
    scale = np.exp2(byte - 127.0)
    codes = (blocks / scale).astype(np.float32).astype(dtype).astype(np.float64)
    return np.moveaxis((codes * scale).reshape(v.shape), -1, axis)


WIDE = False


def mx_kscale(k):
    if not WIDE:
        return np.ones(k)
    levels = np.array([10, -10, 5, -5, 0])
    a = np.random.permutation(np.resize(levels, k // 512 * 4)).reshape(k // 512, 4)
    idx = np.arange(k)
    return np.exp2(a[idx // 512, idx % 128 // 32])


BF16 = ml_dtypes.bfloat16


def bf(x):
    return np.asarray(x, np.float32).astype(BF16)


def f64(x):
    return np.asarray(x).astype(np.float64)


E2M1 = np.array([0.0, 0.5, 1.0, 1.5, 2.0, 3.0, 4.0, 6.0, -0.0, -0.5, -1.0, -1.5, -2.0, -3.0, -4.0, -6.0])


def pack_weight(w, fmt):
    k, n = w.shape
    w = f64(bf(w)).reshape(k // 32, 32, n)
    amax = np.abs(w).max(1)
    if fmt == "e4m3":
        byte = np.frexp(amax)[1] - 1 + 127 - 7
    else:
        mant, ex = np.frexp(amax / 6.0)
        byte = np.where(mant > 0.5, ex, ex - 1) + 127
    byte = np.clip(np.where(amax > 0, byte, 1), 1, 254)
    scaled = (w * np.exp2(127.0 - byte)[:, None, :]).reshape(k, n).astype(np.float32)
    by_word = np.ascontiguousarray(scaled.reshape(k // 512, 128, 4, n).transpose(0, 1, 3, 2))
    if fmt == "e4m3":
        words = by_word.astype(ml_dtypes.float8_e4m3fn).view(np.uint8)
    else:
        c = by_word.astype(ml_dtypes.float4_e2m1fn).view(np.uint8) & 0xF
        words = c[..., 0::2] | (c[..., 1::2] << 4)
    return np.ascontiguousarray(words), np.ascontiguousarray(byte.astype(np.uint8).reshape(k // 512, 16, n))


def unpack_weight(words, scales, fmt):
    g, p, n, _ = words.shape
    if fmt == "e4m3":
        vals = np.ascontiguousarray(words).view(ml_dtypes.float8_e4m3fn).astype(np.float64)
    else:
        nib = np.empty((g, p, n, 4), np.uint8)
        nib[..., 0::2] = words & 0xF
        nib[..., 1::2] = words >> 4
        vals = E2M1[nib]
    vals = vals * np.repeat(np.exp2(scales.astype(np.float64) - 127.0), 8, axis=1)[..., None]
    return vals.transpose(0, 1, 3, 2).reshape(g * 512, n)

def pack4(w):
    words, scales = pack_weight(w, "e2m1")
    return words.reshape(words.shape[0], 128, -1), scales


def unpack4(words, scales):
    return unpack_weight(words.reshape(words.shape[0], 128, -1, 2), scales, "e2m1")


B, N, D, H, DH = 2, 2048, 512, 4, 64
INNER = H * DH


def dpfp(u):
    u2 = np.concatenate([np.maximum(u, 0.0), np.maximum(-u, 0.0)], axis=-1)
    return u2 * np.roll(u2, 1, axis=-1)


def heads(t):
    return t.reshape(B, N, H, DH).transpose(0, 2, 1, 3)


def setup_inputs():
    s = mx_kscale(D)
    x = bf(np.random.standard_normal((B, N, D)) * s)
    words, scales = pack4(np.random.standard_normal((D, 2 * INNER)) / np.sqrt(D) / s[:, None])
    return {"x": x, "w_qk_words": words, "w_qk_scales": scales}


def reference(x, w_qk_words, w_qk_scales):
    qk = mxq(f64(x), 2, "e4m3") @ unpack4(w_qk_words, w_qk_scales)
    q, k = np.split(qk, 2, axis=-1)
    q, k = dpfp(heads(q)), dpfp(heads(k))
    return q / q.sum(-1, keepdims=True), k / k.sum(-1, keepdims=True)

@@ -1,0 +1,206 @@
+from contextlib import ExitStack
+
+import concourse.mybir as mybir
+from concourse.masks import make_identity
+
+F32 = mybir.dt.float32
+BF16 = mybir.dt.bfloat16
+I32 = mybir.dt.int32
+U32 = mybir.dt.uint32
+U8 = mybir.dt.uint8
+FP8X4 = mybir.dt.float8_e4m3fn_x4
+FP4X4 = mybir.dt.float4_e2m1fn_x4
+ALU = mybir.AluOpType
+ACT = mybir.ActivationFunctionType
+
+P = 128
+BATCH, TOKENS, K = 2, 2048, 512
+HEADS, DH = 8, 64
+COLS = HEADS * DH
+GROUP = 4
+GROUPS_PER_BATCH = TOKENS // (P * GROUP)
+TILES = BATCH * TOKENS // P
+PAIR = 2
+WORDS = K // 2
+
+FLOPS = 2 * BATCH * TOKENS * K * COLS
+
+LAG_TRANSPOSE = 0
+LAG_REGROUP = 1
+LAG_QUANTISE = 2
+LAG_PROJECT = 3
+LAG_PRODUCTS = 4
+LAG_SUMS = 5
+LAG_SCALE = 6
+LAG_MASK = 7
+
+
+def tile_dpfpattention_pa_t_kernel(tc, x, w_qk_words, w_qk_scales, out_0, out_1):
+    nc = tc.nc
+    x_groups = x.rearrange("b (p c t) k -> b c p t k", p=P, t=GROUP)
+    q_groups = out_0.rearrange("b h (p c t) f -> b c p h t f", p=P, t=GROUP)
+    k_groups = out_1.rearrange("b h (p c t) f -> b c p h t f", p=P, t=GROUP)
+
+    with ExitStack() as ctx:
+        const = ctx.enter_context(tc.tile_pool(name="const", bufs=1))
+        x_pool = ctx.enter_context(tc.tile_pool(name="x_pool", bufs=TILES // GROUP))
+        quant_pool = ctx.enter_context(tc.tile_pool(name="quant_pool", bufs=3))
+        work = ctx.enter_context(tc.tile_pool(name="work", bufs=3))
+        out_pool = ctx.enter_context(tc.tile_pool(name="out_pool", bufs=3))
+        psum_t = ctx.enter_context(tc.psum_pool(name="psum_t", bufs=2))
+        psum_u = ctx.enter_context(tc.psum_pool(name="psum_u", bufs=6))
+        ctx.enter_context(tc.manual_schedule())
+
+        x_tiles = []
+        for g in range(TILES // GROUP):
+            x_tiles.append(x_pool.tile([P, GROUP, K], BF16, name="x_sb"))
+
+        def load_x(g):
+            b, c = divmod(g, GROUPS_PER_BATCH)
+            nc.sync.dma_start(out=x_tiles[g][:], in_=x_groups[b, c])
+
+        w_plane = const.tile([P, COLS], U8, align_bytes=64)
+        nc.vector.memset(w_plane[:].bitcast(I32), 0)
+        w_words = const.tile([P, 2 * COLS], U8, align_bytes=64)
+
+        load_x(0)
+        nc.sync.dma_start(out=w_words[:].bitcast(I32), in_=w_qk_words[0].bitcast(I32))
+        for quadrant in range(4):
+            nc.sync.dma_start(
+                out=w_plane[32 * quadrant : 32 * quadrant + 4, :].bitcast(I32),
+                in_=w_qk_scales[0, 4 * quadrant : 4 * quadrant + 4, :].bitcast(I32),
+            )
+        for g in range(1, TILES // GROUP):
+            load_x(g)
+
+        identity = const.tile([P, P], F32)
+        make_identity(nc, identity[:])
+
+        xt_of, grouped_of, codes_of, scales_of = {}, {}, {}, {}
+        u_of, prod_of, relu_of, sums_of, scaled_of, phi_of = {}, {}, {}, {}, {}, {}
+
+        def transpose_pair(first):
+            xt = psum_t.tile([P, PAIR, 2, P], F32, name="xt")
+            xt_of[first] = xt
+            for j in range(PAIR):
+                g, t = divmod(first + j, GROUP)
+                words = x_tiles[g][:].bitcast(F32)
+                for half in range(2):
+                    nc.tensor.transpose(xt[:, j, half, :], words[:, t, half:WORDS:2], identity[:])
+
+        def regroup_pair(first):
+            grouped = quant_pool.tile([P, PAIR, P, 4], BF16, name="grouped", align_bytes=64)
+            grouped_of[first] = grouped
+            nc.scalar.copy(
+                out=grouped[:].bitcast(F32),
+                in_=xt_of[first][:].rearrange("p j half r -> p j r half"),
+            )
+
+        def quantise_pair(first):
+            codes = quant_pool.tile([P, PAIR * P], U32, name="codes", align_bytes=64)
+            scales = quant_pool.tile([P, PAIR * P], U8, name="scales", align_bytes=64)
+            codes_of[first], scales_of[first] = codes, scales
+            nc.vector.quantize_mx(
+                out=codes[:].bitcast(FP8X4),
+                scales=scales[:],
+                in_=grouped_of[first][:].rearrange("p j r t -> p (j r t)"),
+            )
+
+        def project(i):
+            first, j = i - i % PAIR, i % PAIR
+            tokens = slice(j * P, (j + 1) * P)
+            u = psum_u.tile([P, HEADS, DH], F32, name="u")
+            u_of[i] = u
+            nc.tensor.matmul_mx(
+                out=u[:].rearrange("p h d -> p (h d)"),
+                lhsT=codes_of[first][:, tokens].bitcast(FP8X4),
+                lhsT_scale=scales_of[first][:, tokens],
+                rhs=w_words[:].bitcast(FP4X4),
+                rhs_scale=w_plane[:],
+                start=True,
+                stop=True,
+            )
+
+        def shift(i):
+            prev = work.tile([P, HEADS, DH], F32, name="prev")
+            nc.scalar.copy(out=prev[:, :, 1:DH], in_=u_of[i][:, :, 0 : DH - 1])
+            nc.scalar.mul(out=prev[:, :, 0:1], in_=u_of[i][:, :, DH - 1 : DH], mul=-1.0)
+            return prev
+
+        def products(i, prev):
+            prod = work.tile([P, HEADS, DH], F32, name="prod")
+            prod_of[i] = prod
+            nc.vector.tensor_tensor(out=prod[:], in0=u_of[i][:], in1=prev[:], op=ALU.mult)
+
+        def sums(i):
+            relu = work.tile([P, HEADS, DH], F32, name="relu")
+            total = work.tile([P, HEADS], F32, name="total")
+            relu_of[i], sums_of[i] = relu, total
+            for h in range(HEADS):
+                nc.scalar.activation(
+                    out=relu[:, h, :],
+                    in_=prod_of[i][:, h, :],
+                    func=ACT.Relu,
+                    accum_out=total[:, h : h + 1],
+                )
+
+        def reciprocal(i):
+            recip = work.tile([P, HEADS], F32, name="recip")
+            nc.vector.reciprocal(recip[:], sums_of[i][:])
+            return recip
+
+        def scale(i, recip):
+            scaled = work.tile([P, HEADS, DH], F32, name="scaled")
+            scaled_of[i] = scaled
+            for h in range(HEADS):
+                nc.vector.tensor_scalar(
+                    out=scaled[:, h, :],
+                    in0=relu_of[i][:, h, :],
+                    scalar1=recip[:, h : h + 1],
+                    scalar2=None,
+                    op0=ALU.mult,
+                )
+
+        def mask_and_store(i):
+            g, t = divmod(i, GROUP)
+            if t == 0:
+                phi_of[g] = out_pool.tile([P, HEADS, GROUP, 2 * DH], F32, name="phi")
+            phi = phi_of[g]
+            nc.vector.scalar_tensor_tensor(
+                out=phi[:, :, t, 0:DH], in0=u_of[i][:], scalar=0.0, in1=scaled_of[i][:],
+                op0=ALU.is_gt, op1=ALU.mult,
+            )
+            nc.gpsimd.tensor_tensor(
+                out=phi[:, :, t, DH : 2 * DH], in0=scaled_of[i][:], in1=phi[:, :, t, 0:DH],
+                op=ALU.subtract,
+            )
+            if t == GROUP - 1:
+                b, c = divmod(g, GROUPS_PER_BATCH)
+                nc.sync.dma_start(out=q_groups[b, c], in_=phi[:, 0 : HEADS // 2])
+                nc.sync.dma_start(out=k_groups[b, c], in_=phi[:, HEADS // 2 : HEADS])
+
+        def due(step, lag, every=1):
+            i = step - lag
+            return 0 <= i < TILES and i % every == 0
+
+        for step in range(TILES + LAG_MASK):
+            if due(step, LAG_TRANSPOSE, PAIR):
+                transpose_pair(step - LAG_TRANSPOSE)
+            if due(step, LAG_PROJECT):
+                project(step - LAG_PROJECT)
+            if due(step, LAG_PRODUCTS):
+                prev = shift(step - LAG_PRODUCTS)
+            if due(step, LAG_SCALE):
+                recip = reciprocal(step - LAG_SCALE)
+            if due(step, LAG_MASK):
+                mask_and_store(step - LAG_MASK)
+            if due(step, LAG_REGROUP, PAIR):
+                regroup_pair(step - LAG_REGROUP)
+            if due(step, LAG_SCALE):
+                scale(step - LAG_SCALE, recip)
+            if due(step, LAG_PRODUCTS):
+                products(step - LAG_PRODUCTS, prev)
+            if due(step, LAG_QUANTISE, PAIR):
+                quantise_pair(step - LAG_QUANTISE)
+            if due(step, LAG_SUMS):
+                sums(step - LAG_SUMS)

@@ -170,9 +170,9 @@ def tile_dpfpattention_pa_t_kernel(tc, x, w_qk_words, w_qk_scales, out_0, out_1)
                 out=phi[:, :, t, 0:DH], in0=u_of[i][:], scalar=0.0, in1=scaled_of[i][:],
                 op0=ALU.is_gt, op1=ALU.mult,
             )
-            nc.gpsimd.tensor_tensor(
-                out=phi[:, :, t, DH : 2 * DH], in0=scaled_of[i][:], in1=phi[:, :, t, 0:DH],
-                op=ALU.subtract,
+            nc.vector.scalar_tensor_tensor(
+                out=phi[:, :, t, DH : 2 * DH], in0=u_of[i][:], scalar=0.0, in1=scaled_of[i][:],
+                op0=ALU.is_lt, op1=ALU.mult,
             )
             if t == GROUP - 1:
                 b, c = divmod(g, GROUPS_PER_BATCH)

@@ -17,10 +17,11 @@ P = 128
 BATCH, TOKENS, K = 2, 2048, 512
 HEADS, DH = 8, 64
 COLS = HEADS * DH
-GROUP = 4
-GROUPS_PER_BATCH = TOKENS // (P * GROUP)
 TILES = BATCH * TOKENS // P
 PAIR = 2
+PAIRS_PER_BATCH = TOKENS // (P * PAIR)
+GROUP = 4
+GROUPS_PER_BATCH = TOKENS // (P * GROUP)
 WORDS = K // 2
 
 FLOPS = 2 * BATCH * TOKENS * K * COLS
@@ -37,13 +38,13 @@ LAG_MASK = 7
 
 def tile_dpfpattention_pa_t_kernel(tc, x, w_qk_words, w_qk_scales, out_0, out_1):
     nc = tc.nc
-    x_groups = x.rearrange("b (p c t) k -> b c p t k", p=P, t=GROUP)
+    x_pairs = x.rearrange("b (p c t) k -> b c p t k", p=P, t=PAIR)
     q_groups = out_0.rearrange("b h (p c t) f -> b c p h t f", p=P, t=GROUP)
     k_groups = out_1.rearrange("b h (p c t) f -> b c p h t f", p=P, t=GROUP)
 
     with ExitStack() as ctx:
         const = ctx.enter_context(tc.tile_pool(name="const", bufs=1))
-        x_pool = ctx.enter_context(tc.tile_pool(name="x_pool", bufs=TILES // GROUP))
+        x_pool = ctx.enter_context(tc.tile_pool(name="x_pool", bufs=TILES // PAIR))
         quant_pool = ctx.enter_context(tc.tile_pool(name="quant_pool", bufs=3))
         work = ctx.enter_context(tc.tile_pool(name="work", bufs=3))
         out_pool = ctx.enter_context(tc.tile_pool(name="out_pool", bufs=3))
@@ -52,12 +53,12 @@ def tile_dpfpattention_pa_t_kernel(tc, x, w_qk_words, w_qk_scales, out_0, out_1)
         ctx.enter_context(tc.manual_schedule())
 
         x_tiles = []
-        for g in range(TILES // GROUP):
-            x_tiles.append(x_pool.tile([P, GROUP, K], BF16, name="x_sb"))
+        for pair in range(TILES // PAIR):
+            x_tiles.append(x_pool.tile([P, PAIR, K], BF16, name="x_sb"))
 
-        def load_x(g):
-            b, c = divmod(g, GROUPS_PER_BATCH)
-            nc.sync.dma_start(out=x_tiles[g][:], in_=x_groups[b, c])
+        def load_x(pair):
+            b, c = divmod(pair, PAIRS_PER_BATCH)
+            nc.sync.dma_start(out=x_tiles[pair][:], in_=x_pairs[b, c])
 
         w_plane = const.tile([P, COLS], U8, align_bytes=64)
         nc.vector.memset(w_plane[:].bitcast(I32), 0)
@@ -70,8 +71,8 @@ def tile_dpfpattention_pa_t_kernel(tc, x, w_qk_words, w_qk_scales, out_0, out_1)
                 out=w_plane[32 * quadrant : 32 * quadrant + 4, :].bitcast(I32),
                 in_=w_qk_scales[0, 4 * quadrant : 4 * quadrant + 4, :].bitcast(I32),
             )
-        for g in range(1, TILES // GROUP):
-            load_x(g)
+        for pair in range(1, TILES // PAIR):
+            load_x(pair)
 
         identity = const.tile([P, P], F32)
         make_identity(nc, identity[:])
@@ -82,19 +83,19 @@ def tile_dpfpattention_pa_t_kernel(tc, x, w_qk_words, w_qk_scales, out_0, out_1)
         def transpose_pair(first):
             xt = psum_t.tile([P, PAIR, 2, P], F32, name="xt")
             xt_of[first] = xt
+            words = x_tiles[first // PAIR][:].bitcast(F32)
             for j in range(PAIR):
-                g, t = divmod(first + j, GROUP)
-                words = x_tiles[g][:].bitcast(F32)
                 for half in range(2):
-                    nc.tensor.transpose(xt[:, j, half, :], words[:, t, half:WORDS:2], identity[:])
+                    nc.tensor.transpose(xt[:, j, half, :], words[:, j, half:WORDS:2], identity[:])
 
         def regroup_pair(first):
             grouped = quant_pool.tile([P, PAIR, P, 4], BF16, name="grouped", align_bytes=64)
             grouped_of[first] = grouped
-            nc.scalar.copy(
-                out=grouped[:].bitcast(F32),
-                in_=xt_of[first][:].rearrange("p j half r -> p j r half"),
-            )
+            by_token = xt_of[first][:].rearrange("p j half r -> p j r half")
+            if (first // PAIR) % 2 == 0:
+                nc.scalar.copy(out=grouped[:].bitcast(F32), in_=by_token)
+            else:
+                nc.vector.tensor_copy(out=grouped[:].bitcast(F32), in_=by_token)
 
         def quantise_pair(first):
             codes = quant_pool.tile([P, PAIR * P], U32, name="codes", align_bytes=64)
@@ -170,12 +171,15 @@ def tile_dpfpattention_pa_t_kernel(tc, x, w_qk_words, w_qk_scales, out_0, out_1)
                 out=phi[:, :, t, 0:DH], in0=u_of[i][:], scalar=0.0, in1=scaled_of[i][:],
                 op0=ALU.is_gt, op1=ALU.mult,
             )
-            nc.vector.scalar_tensor_tensor(
-                out=phi[:, :, t, DH : 2 * DH], in0=u_of[i][:], scalar=0.0, in1=scaled_of[i][:],
-                op0=ALU.is_lt, op1=ALU.mult,
+            nc.gpsimd.tensor_tensor(
+                out=phi[:, :, t, DH : 2 * DH], in0=scaled_of[i][:], in1=phi[:, :, t, 0:DH],
+                op=ALU.subtract,
             )
-            if t == GROUP - 1:
-                b, c = divmod(g, GROUPS_PER_BATCH)
+            b, c = divmod(g, GROUPS_PER_BATCH)
+            if g == TILES // GROUP - 1:
+                nc.sync.dma_start(out=q_groups[b, c][:, :, t, :], in_=phi[:, 0 : HEADS // 2, t, :])
+                nc.sync.dma_start(out=k_groups[b, c][:, :, t, :], in_=phi[:, HEADS // 2 : HEADS, t, :])
+            elif t == GROUP - 1:
                 nc.sync.dma_start(out=q_groups[b, c], in_=phi[:, 0 : HEADS // 2])
                 nc.sync.dma_start(out=k_groups[b, c], in_=phi[:, HEADS // 2 : HEADS])
 

@@ -17,11 +17,10 @@ P = 128
 BATCH, TOKENS, K = 2, 2048, 512
 HEADS, DH = 8, 64
 COLS = HEADS * DH
-TILES = BATCH * TOKENS // P
-PAIR = 2
-PAIRS_PER_BATCH = TOKENS // (P * PAIR)
 GROUP = 4
 GROUPS_PER_BATCH = TOKENS // (P * GROUP)
+TILES = BATCH * TOKENS // P
+PAIR = 2
 WORDS = K // 2
 
 FLOPS = 2 * BATCH * TOKENS * K * COLS
@@ -30,35 +29,36 @@ LAG_TRANSPOSE = 0
 LAG_REGROUP = 1
 LAG_QUANTISE = 2
 LAG_PROJECT = 3
-LAG_PRODUCTS = 4
-LAG_SUMS = 5
-LAG_SCALE = 6
-LAG_MASK = 7
+LAG_SHIFT = 4
+LAG_PRODUCTS = 5
+LAG_SUMS = 6
+LAG_SCALE = 7
+LAG_MASK = 9
 
 
 def tile_dpfpattention_pa_t_kernel(tc, x, w_qk_words, w_qk_scales, out_0, out_1):
     nc = tc.nc
-    x_pairs = x.rearrange("b (p c t) k -> b c p t k", p=P, t=PAIR)
+    x_groups = x.rearrange("b (p c t) k -> b c p t k", p=P, t=GROUP)
     q_groups = out_0.rearrange("b h (p c t) f -> b c p h t f", p=P, t=GROUP)
     k_groups = out_1.rearrange("b h (p c t) f -> b c p h t f", p=P, t=GROUP)
 
     with ExitStack() as ctx:
         const = ctx.enter_context(tc.tile_pool(name="const", bufs=1))
-        x_pool = ctx.enter_context(tc.tile_pool(name="x_pool", bufs=TILES // PAIR))
+        x_pool = ctx.enter_context(tc.tile_pool(name="x_pool", bufs=TILES // GROUP))
         quant_pool = ctx.enter_context(tc.tile_pool(name="quant_pool", bufs=3))
-        work = ctx.enter_context(tc.tile_pool(name="work", bufs=3))
+        work = ctx.enter_context(tc.tile_pool(name="work", bufs=4))
         out_pool = ctx.enter_context(tc.tile_pool(name="out_pool", bufs=3))
-        psum_t = ctx.enter_context(tc.psum_pool(name="psum_t", bufs=2))
-        psum_u = ctx.enter_context(tc.psum_pool(name="psum_u", bufs=6))
+        psum_t = ctx.enter_context(tc.psum_pool(name="psum_t", bufs=1))
+        psum_u = ctx.enter_context(tc.psum_pool(name="psum_u", bufs=7))
         ctx.enter_context(tc.manual_schedule())
 
         x_tiles = []
-        for pair in range(TILES // PAIR):
-            x_tiles.append(x_pool.tile([P, PAIR, K], BF16, name="x_sb"))
+        for g in range(TILES // GROUP):
+            x_tiles.append(x_pool.tile([P, GROUP, K], BF16, name="x_sb"))
 
-        def load_x(pair):
-            b, c = divmod(pair, PAIRS_PER_BATCH)
-            nc.sync.dma_start(out=x_tiles[pair][:], in_=x_pairs[b, c])
+        def load_x(g):
+            b, c = divmod(g, GROUPS_PER_BATCH)
+            nc.sync.dma_start(out=x_tiles[g][:], in_=x_groups[b, c])
 
         w_plane = const.tile([P, COLS], U8, align_bytes=64)
         nc.vector.memset(w_plane[:].bitcast(I32), 0)
@@ -71,31 +71,31 @@ def tile_dpfpattention_pa_t_kernel(tc, x, w_qk_words, w_qk_scales, out_0, out_1)
                 out=w_plane[32 * quadrant : 32 * quadrant + 4, :].bitcast(I32),
                 in_=w_qk_scales[0, 4 * quadrant : 4 * quadrant + 4, :].bitcast(I32),
             )
-        for pair in range(1, TILES // PAIR):
-            load_x(pair)
+        for g in range(1, TILES // GROUP):
+            load_x(g)
 
         identity = const.tile([P, P], F32)
         make_identity(nc, identity[:])
 
         xt_of, grouped_of, codes_of, scales_of = {}, {}, {}, {}
-        u_of, prod_of, relu_of, sums_of, scaled_of, phi_of = {}, {}, {}, {}, {}, {}
+        u_of, prev_of, prod_of, relu_of, sums_of, scaled_of, phi_of = {}, {}, {}, {}, {}, {}, {}
 
         def transpose_pair(first):
             xt = psum_t.tile([P, PAIR, 2, P], F32, name="xt")
             xt_of[first] = xt
-            words = x_tiles[first // PAIR][:].bitcast(F32)
             for j in range(PAIR):
+                g, t = divmod(first + j, GROUP)
+                words = x_tiles[g][:].bitcast(F32)
                 for half in range(2):
-                    nc.tensor.transpose(xt[:, j, half, :], words[:, j, half:WORDS:2], identity[:])
+                    nc.tensor.transpose(xt[:, j, half, :], words[:, t, half:WORDS:2], identity[:])
 
         def regroup_pair(first):
             grouped = quant_pool.tile([P, PAIR, P, 4], BF16, name="grouped", align_bytes=64)
             grouped_of[first] = grouped
-            by_token = xt_of[first][:].rearrange("p j half r -> p j r half")
-            if (first // PAIR) % 2 == 0:
-                nc.scalar.copy(out=grouped[:].bitcast(F32), in_=by_token)
-            else:
-                nc.vector.tensor_copy(out=grouped[:].bitcast(F32), in_=by_token)
+            nc.scalar.copy(
+                out=grouped[:].bitcast(F32),
+                in_=xt_of[first][:].rearrange("p j half r -> p j r half"),
+            )
 
         def quantise_pair(first):
             codes = quant_pool.tile([P, PAIR * P], U32, name="codes", align_bytes=64)
@@ -124,14 +124,14 @@ def tile_dpfpattention_pa_t_kernel(tc, x, w_qk_words, w_qk_scales, out_0, out_1)
 
         def shift(i):
             prev = work.tile([P, HEADS, DH], F32, name="prev")
+            prev_of[i] = prev
             nc.scalar.copy(out=prev[:, :, 1:DH], in_=u_of[i][:, :, 0 : DH - 1])
             nc.scalar.mul(out=prev[:, :, 0:1], in_=u_of[i][:, :, DH - 1 : DH], mul=-1.0)
-            return prev
 
-        def products(i, prev):
+        def products(i):
             prod = work.tile([P, HEADS, DH], F32, name="prod")
             prod_of[i] = prod
-            nc.vector.tensor_tensor(out=prod[:], in0=u_of[i][:], in1=prev[:], op=ALU.mult)
+            nc.vector.tensor_tensor(out=prod[:], in0=u_of[i][:], in1=prev_of[i][:], op=ALU.mult)
 
         def sums(i):
             relu = work.tile([P, HEADS, DH], F32, name="relu")
@@ -145,22 +145,17 @@ def tile_dpfpattention_pa_t_kernel(tc, x, w_qk_words, w_qk_scales, out_0, out_1)
                     accum_out=total[:, h : h + 1],
                 )
 
-        def reciprocal(i):
+        def scale(i):
             recip = work.tile([P, HEADS], F32, name="recip")
             nc.vector.reciprocal(recip[:], sums_of[i][:])
-            return recip
-
-        def scale(i, recip):
             scaled = work.tile([P, HEADS, DH], F32, name="scaled")
             scaled_of[i] = scaled
-            for h in range(HEADS):
-                nc.vector.tensor_scalar(
-                    out=scaled[:, h, :],
-                    in0=relu_of[i][:, h, :],
-                    scalar1=recip[:, h : h + 1],
-                    scalar2=None,
-                    op0=ALU.mult,
-                )
+            nc.gpsimd.tensor_tensor(
+                out=scaled[:],
+                in0=relu_of[i][:],
+                in1=recip[:].unsqueeze(2).to_broadcast([P, HEADS, DH]),
+                op=ALU.mult,
+            )
 
         def mask_and_store(i):
             g, t = divmod(i, GROUP)
@@ -171,15 +166,12 @@ def tile_dpfpattention_pa_t_kernel(tc, x, w_qk_words, w_qk_scales, out_0, out_1)
                 out=phi[:, :, t, 0:DH], in0=u_of[i][:], scalar=0.0, in1=scaled_of[i][:],
                 op0=ALU.is_gt, op1=ALU.mult,
             )
-            nc.gpsimd.tensor_tensor(
-                out=phi[:, :, t, DH : 2 * DH], in0=scaled_of[i][:], in1=phi[:, :, t, 0:DH],
-                op=ALU.subtract,
+            nc.vector.scalar_tensor_tensor(
+                out=phi[:, :, t, DH : 2 * DH], in0=u_of[i][:], scalar=0.0, in1=scaled_of[i][:],
+                op0=ALU.is_lt, op1=ALU.mult,
             )
-            b, c = divmod(g, GROUPS_PER_BATCH)
-            if g == TILES // GROUP - 1:
-                nc.sync.dma_start(out=q_groups[b, c][:, :, t, :], in_=phi[:, 0 : HEADS // 2, t, :])
-                nc.sync.dma_start(out=k_groups[b, c][:, :, t, :], in_=phi[:, HEADS // 2 : HEADS, t, :])
-            elif t == GROUP - 1:
+            if t == GROUP - 1:
+                b, c = divmod(g, GROUPS_PER_BATCH)
                 nc.sync.dma_start(out=q_groups[b, c], in_=phi[:, 0 : HEADS // 2])
                 nc.sync.dma_start(out=k_groups[b, c], in_=phi[:, HEADS // 2 : HEADS])
 
@@ -192,19 +184,17 @@ def tile_dpfpattention_pa_t_kernel(tc, x, w_qk_words, w_qk_scales, out_0, out_1)
                 transpose_pair(step - LAG_TRANSPOSE)
             if due(step, LAG_PROJECT):
                 project(step - LAG_PROJECT)
+            if due(step, LAG_SHIFT):
+                shift(step - LAG_SHIFT)
             if due(step, LAG_PRODUCTS):
-                prev = shift(step - LAG_PRODUCTS)
-            if due(step, LAG_SCALE):
-                recip = reciprocal(step - LAG_SCALE)
-            if due(step, LAG_MASK):
-                mask_and_store(step - LAG_MASK)
+                products(step - LAG_PRODUCTS)
             if due(step, LAG_REGROUP, PAIR):
                 regroup_pair(step - LAG_REGROUP)
-            if due(step, LAG_SCALE):
-                scale(step - LAG_SCALE, recip)
-            if due(step, LAG_PRODUCTS):
-                products(step - LAG_PRODUCTS, prev)
-            if due(step, LAG_QUANTISE, PAIR):
-                quantise_pair(step - LAG_QUANTISE)
+            if due(step, LAG_MASK):
+                mask_and_store(step - LAG_MASK)
             if due(step, LAG_SUMS):
                 sums(step - LAG_SUMS)
+            if due(step, LAG_QUANTISE, PAIR):
+                quantise_pair(step - LAG_QUANTISE)
+            if due(step, LAG_SCALE):
+                scale(step - LAG_SCALE)

@@ -32,8 +32,8 @@ LAG_PROJECT = 3
 LAG_SHIFT = 4
 LAG_PRODUCTS = 5
 LAG_SUMS = 6
-LAG_SCALE = 7
-LAG_MASK = 9
+LAG_SCALE = 6
+LAG_MASK = 8
 
 
 def tile_dpfpattention_pa_t_kernel(tc, x, w_qk_words, w_qk_scales, out_0, out_1):
@@ -41,6 +41,8 @@ def tile_dpfpattention_pa_t_kernel(tc, x, w_qk_words, w_qk_scales, out_0, out_1)
     x_groups = x.rearrange("b (p c t) k -> b c p t k", p=P, t=GROUP)
     q_groups = out_0.rearrange("b h (p c t) f -> b c p h t f", p=P, t=GROUP)
     k_groups = out_1.rearrange("b h (p c t) f -> b c p h t f", p=P, t=GROUP)
+    q_tiles = out_0.rearrange("b h (p c t) f -> b c t p h f", p=P, t=GROUP)
+    k_tiles = out_1.rearrange("b h (p c t) f -> b c t p h f", p=P, t=GROUP)
 
     with ExitStack() as ctx:
         const = ctx.enter_context(tc.tile_pool(name="const", bufs=1))
@@ -64,13 +66,14 @@ def tile_dpfpattention_pa_t_kernel(tc, x, w_qk_words, w_qk_scales, out_0, out_1)
         nc.vector.memset(w_plane[:].bitcast(I32), 0)
         w_words = const.tile([P, 2 * COLS], U8, align_bytes=64)
 
-        load_x(0)
+        nc.sync.dma_start(out=x_tiles[0][:, 0:PAIR, :], in_=x_groups[0, 0][:, 0:PAIR, :])
         nc.sync.dma_start(out=w_words[:].bitcast(I32), in_=w_qk_words[0].bitcast(I32))
         for quadrant in range(4):
             nc.sync.dma_start(
                 out=w_plane[32 * quadrant : 32 * quadrant + 4, :].bitcast(I32),
                 in_=w_qk_scales[0, 4 * quadrant : 4 * quadrant + 4, :].bitcast(I32),
             )
+        nc.sync.dma_start(out=x_tiles[0][:, PAIR:GROUP, :], in_=x_groups[0, 0][:, PAIR:GROUP, :])
         for g in range(1, TILES // GROUP):
             load_x(g)
 
@@ -170,8 +173,11 @@ def tile_dpfpattention_pa_t_kernel(tc, x, w_qk_words, w_qk_scales, out_0, out_1)
                 out=phi[:, :, t, DH : 2 * DH], in0=u_of[i][:], scalar=0.0, in1=scaled_of[i][:],
                 op0=ALU.is_lt, op1=ALU.mult,
             )
-            if t == GROUP - 1:
-                b, c = divmod(g, GROUPS_PER_BATCH)
+            b, c = divmod(g, GROUPS_PER_BATCH)
+            if g == TILES // GROUP - 1:
+                nc.sync.dma_start(out=q_tiles[b, c, t], in_=phi[:, 0 : HEADS // 2, t, :])
+                nc.sync.dma_start(out=k_tiles[b, c, t], in_=phi[:, HEADS // 2 : HEADS, t, :])
+            elif t == GROUP - 1:
                 nc.sync.dma_start(out=q_groups[b, c], in_=phi[:, 0 : HEADS // 2])
                 nc.sync.dma_start(out=k_groups[b, c], in_=phi[:, HEADS // 2 : HEADS])
 

@@ -41,8 +41,6 @@ def tile_dpfpattention_pa_t_kernel(tc, x, w_qk_words, w_qk_scales, out_0, out_1)
     x_groups = x.rearrange("b (p c t) k -> b c p t k", p=P, t=GROUP)
     q_groups = out_0.rearrange("b h (p c t) f -> b c p h t f", p=P, t=GROUP)
     k_groups = out_1.rearrange("b h (p c t) f -> b c p h t f", p=P, t=GROUP)
-    q_tiles = out_0.rearrange("b h (p c t) f -> b c t p h f", p=P, t=GROUP)
-    k_tiles = out_1.rearrange("b h (p c t) f -> b c t p h f", p=P, t=GROUP)
 
     with ExitStack() as ctx:
         const = ctx.enter_context(tc.tile_pool(name="const", bufs=1))
@@ -173,11 +171,8 @@ def tile_dpfpattention_pa_t_kernel(tc, x, w_qk_words, w_qk_scales, out_0, out_1)
                 out=phi[:, :, t, DH : 2 * DH], in0=u_of[i][:], scalar=0.0, in1=scaled_of[i][:],
                 op0=ALU.is_lt, op1=ALU.mult,
             )
-            b, c = divmod(g, GROUPS_PER_BATCH)
-            if g == TILES // GROUP - 1:
-                nc.sync.dma_start(out=q_tiles[b, c, t], in_=phi[:, 0 : HEADS // 2, t, :])
-                nc.sync.dma_start(out=k_tiles[b, c, t], in_=phi[:, HEADS // 2 : HEADS, t, :])
-            elif t == GROUP - 1:
+            if t == GROUP - 1:
+                b, c = divmod(g, GROUPS_PER_BATCH)
                 nc.sync.dma_start(out=q_groups[b, c], in_=phi[:, 0 : HEADS // 2])
                 nc.sync.dma_start(out=k_groups[b, c], in_=phi[:, HEADS // 2 : HEADS])
 

@@ -38,9 +38,9 @@ LAG_MASK = 8
 
 def tile_dpfpattention_pa_t_kernel(tc, x, w_qk_words, w_qk_scales, out_0, out_1):
     nc = tc.nc
-    x_groups = x.rearrange("b (p c t) k -> b c p t k", p=P, t=GROUP)
-    q_groups = out_0.rearrange("b h (p c t) f -> b c p h t f", p=P, t=GROUP)
-    k_groups = out_1.rearrange("b h (p c t) f -> b c p h t f", p=P, t=GROUP)
+    x_groups = x.rearrange("b (c p t) k -> b c p t k", p=P, t=GROUP)
+    q_groups = out_0.rearrange("b h (c p t) f -> b c p h t f", p=P, t=GROUP)
+    k_groups = out_1.rearrange("b h (c p t) f -> b c p h t f", p=P, t=GROUP)
 
     with ExitStack() as ctx:
         const = ctx.enter_context(tc.tile_pool(name="const", bufs=1))

@@ -126,8 +126,14 @@ def tile_dpfpattention_pa_t_kernel(tc, x, w_qk_words, w_qk_scales, out_0, out_1)
         def shift(i):
             prev = work.tile([P, HEADS, DH], F32, name="prev")
             prev_of[i] = prev
-            nc.scalar.copy(out=prev[:, :, 1:DH], in_=u_of[i][:, :, 0 : DH - 1])
-            nc.scalar.mul(out=prev[:, :, 0:1], in_=u_of[i][:, :, DH - 1 : DH], mul=-1.0)
+            if i + LAG_SHIFT < LAG_MASK:
+                nc.vector.tensor_copy(out=prev[:, :, 1:DH], in_=u_of[i][:, :, 0 : DH - 1])
+                nc.vector.tensor_scalar_mul(
+                    out=prev[:, :, 0:1], in0=u_of[i][:, :, DH - 1 : DH], scalar1=-1.0
+                )
+            else:
+                nc.scalar.copy(out=prev[:, :, 1:DH], in_=u_of[i][:, :, 0 : DH - 1])
+                nc.scalar.mul(out=prev[:, :, 0:1], in_=u_of[i][:, :, DH - 1 : DH], mul=-1.0)
 
         def products(i):
             prod = work.tile([P, HEADS, DH], F32, name="prod")
@@ -171,8 +177,13 @@ def tile_dpfpattention_pa_t_kernel(tc, x, w_qk_words, w_qk_scales, out_0, out_1)
                 out=phi[:, :, t, DH : 2 * DH], in0=u_of[i][:], scalar=0.0, in1=scaled_of[i][:],
                 op0=ALU.is_lt, op1=ALU.mult,
             )
-            if t == GROUP - 1:
-                b, c = divmod(g, GROUPS_PER_BATCH)
+            b, c = divmod(g, GROUPS_PER_BATCH)
+            if g == TILES // GROUP - 1:
+                if t % PAIR == PAIR - 1:
+                    done = slice(t - 1, t + 1)
+                    nc.sync.dma_start(out=q_groups[b, c][:, :, done, :], in_=phi[:, 0 : HEADS // 2, done, :])
+                    nc.sync.dma_start(out=k_groups[b, c][:, :, done, :], in_=phi[:, HEADS // 2 : HEADS, done, :])
+            elif t == GROUP - 1:
                 nc.sync.dma_start(out=q_groups[b, c], in_=phi[:, 0 : HEADS // 2])
                 nc.sync.dma_start(out=k_groups[b, c], in_=phi[:, HEADS // 2 : HEADS])
 

@@ -34,6 +34,7 @@ LAG_PRODUCTS = 5
 LAG_SUMS = 6
 LAG_SCALE = 6
 LAG_MASK = 8
+POOL_HEADS = 1
 
 
 def tile_dpfpattention_pa_t_kernel(tc, x, w_qk_words, w_qk_scales, out_0, out_1):
@@ -173,9 +174,14 @@ def tile_dpfpattention_pa_t_kernel(tc, x, w_qk_words, w_qk_scales, out_0, out_1)
                 out=phi[:, :, t, 0:DH], in0=u_of[i][:], scalar=0.0, in1=scaled_of[i][:],
                 op0=ALU.is_gt, op1=ALU.mult,
             )
+            mine = HEADS - POOL_HEADS
+            nc.gpsimd.tensor_tensor(
+                out=phi[:, mine:HEADS, t, DH : 2 * DH], in0=scaled_of[i][:, mine:HEADS, :],
+                in1=phi[:, mine:HEADS, t, 0:DH], op=ALU.subtract,
+            )
             nc.vector.scalar_tensor_tensor(
-                out=phi[:, :, t, DH : 2 * DH], in0=u_of[i][:], scalar=0.0, in1=scaled_of[i][:],
-                op0=ALU.is_lt, op1=ALU.mult,
+                out=phi[:, 0:mine, t, DH : 2 * DH], in0=u_of[i][:, 0:mine, :], scalar=0.0,
+                in1=scaled_of[i][:, 0:mine, :], op0=ALU.is_lt, op1=ALU.mult,
             )
             b, c = divmod(g, GROUPS_PER_BATCH)
             if g == TILES // GROUP - 1:

@@ -35,6 +35,7 @@ LAG_SUMS = 6
 LAG_SCALE = 6
 LAG_MASK = 8
 POOL_HEADS = 1
+HALVED_GROUPS = 2
 
 
 def tile_dpfpattention_pa_t_kernel(tc, x, w_qk_words, w_qk_scales, out_0, out_1):
@@ -184,7 +185,7 @@ def tile_dpfpattention_pa_t_kernel(tc, x, w_qk_words, w_qk_scales, out_0, out_1)
                 in1=scaled_of[i][:, 0:mine, :], op0=ALU.is_lt, op1=ALU.mult,
             )
             b, c = divmod(g, GROUPS_PER_BATCH)
-            if g == TILES // GROUP - 1:
+            if g >= TILES // GROUP - HALVED_GROUPS:
                 if t % PAIR == PAIR - 1:
                     done = slice(t - 1, t + 1)
                     nc.sync.dma_start(out=q_groups[b, c][:, :, done, :], in_=phi[:, 0 : HEADS // 2, done, :])

@@ -66,7 +66,8 @@ def tile_dpfpattention_pa_t_kernel(tc, x, w_qk_words, w_qk_scales, out_0, out_1)
         nc.vector.memset(w_plane[:].bitcast(I32), 0)
         w_words = const.tile([P, 2 * COLS], U8, align_bytes=64)
 
-        nc.sync.dma_start(out=x_tiles[0][:, 0:PAIR, :], in_=x_groups[0, 0][:, 0:PAIR, :])
+        nc.sync.dma_start(out=x_tiles[0][:, 0:1, :], in_=x_groups[0, 0][:, 0:1, :])
+        nc.sync.dma_start(out=x_tiles[0][:, 1:PAIR, :], in_=x_groups[0, 0][:, 1:PAIR, :])
         nc.sync.dma_start(out=w_words[:].bitcast(I32), in_=w_qk_words[0].bitcast(I32))
         for quadrant in range(4):
             nc.sync.dma_start(
@@ -95,6 +96,13 @@ def tile_dpfpattention_pa_t_kernel(tc, x, w_qk_words, w_qk_scales, out_0, out_1)
         def regroup_pair(first):
             grouped = quant_pool.tile([P, PAIR, P, 4], BF16, name="grouped", align_bytes=64)
             grouped_of[first] = grouped
+            if first == 0:
+                for j in range(PAIR):
+                    nc.scalar.copy(
+                        out=grouped[:, j, :, :].bitcast(F32),
+                        in_=xt_of[first][:, j, :, :].rearrange("p half r -> p r half"),
+                    )
+                return
             nc.scalar.copy(
                 out=grouped[:].bitcast(F32),
                 in_=xt_of[first][:].rearrange("p j half r -> p j r half"),
@@ -104,6 +112,15 @@ def tile_dpfpattention_pa_t_kernel(tc, x, w_qk_words, w_qk_scales, out_0, out_1)
             codes = quant_pool.tile([P, PAIR * P], U32, name="codes", align_bytes=64)
             scales = quant_pool.tile([P, PAIR * P], U8, name="scales", align_bytes=64)
             codes_of[first], scales_of[first] = codes, scales
+            if first == 0:
+                for j in range(PAIR):
+                    tokens = slice(j * P, (j + 1) * P)
+                    nc.vector.quantize_mx(
+                        out=codes[:, tokens].bitcast(FP8X4),
+                        scales=scales[:, tokens],
+                        in_=grouped_of[first][:, j, :, :].rearrange("p r t -> p (r t)"),
+                    )
+                return
             nc.vector.quantize_mx(
                 out=codes[:].bitcast(FP8X4),
                 scales=scales[:],
@@ -166,33 +183,47 @@ def tile_dpfpattention_pa_t_kernel(tc, x, w_qk_words, w_qk_scales, out_0, out_1)
                 op=ALU.mult,
             )
 
+        def masks(i, lo, hi):
+            g, t = divmod(i, GROUP)
+            phi = phi_of[g]
+            nc.vector.scalar_tensor_tensor(
+                out=phi[:, lo:hi, t, 0:DH], in0=u_of[i][:, lo:hi, :], scalar=0.0,
+                in1=scaled_of[i][:, lo:hi, :], op0=ALU.is_gt, op1=ALU.mult,
+            )
+            mine = min(hi, HEADS - POOL_HEADS)
+            if mine < hi:
+                nc.gpsimd.tensor_tensor(
+                    out=phi[:, mine:hi, t, DH : 2 * DH], in0=scaled_of[i][:, mine:hi, :],
+                    in1=phi[:, mine:hi, t, 0:DH], op=ALU.subtract,
+                )
+            nc.vector.scalar_tensor_tensor(
+                out=phi[:, lo:mine, t, DH : 2 * DH], in0=u_of[i][:, lo:mine, :], scalar=0.0,
+                in1=scaled_of[i][:, lo:mine, :], op0=ALU.is_lt, op1=ALU.mult,
+            )
+
         def mask_and_store(i):
             g, t = divmod(i, GROUP)
             if t == 0:
                 phi_of[g] = out_pool.tile([P, HEADS, GROUP, 2 * DH], F32, name="phi")
             phi = phi_of[g]
-            nc.vector.scalar_tensor_tensor(
-                out=phi[:, :, t, 0:DH], in0=u_of[i][:], scalar=0.0, in1=scaled_of[i][:],
-                op0=ALU.is_gt, op1=ALU.mult,
-            )
-            mine = HEADS - POOL_HEADS
-            nc.gpsimd.tensor_tensor(
-                out=phi[:, mine:HEADS, t, DH : 2 * DH], in0=scaled_of[i][:, mine:HEADS, :],
-                in1=phi[:, mine:HEADS, t, 0:DH], op=ALU.subtract,
-            )
-            nc.vector.scalar_tensor_tensor(
-                out=phi[:, 0:mine, t, DH : 2 * DH], in0=u_of[i][:, 0:mine, :], scalar=0.0,
-                in1=scaled_of[i][:, 0:mine, :], op0=ALU.is_lt, op1=ALU.mult,
-            )
             b, c = divmod(g, GROUPS_PER_BATCH)
+            keys = HEADS // 2
+            if i == TILES - 1:
+                done = slice(t - 1, t + 1)
+                masks(i, keys, HEADS)
+                nc.sync.dma_start(out=k_groups[b, c][:, :, done, :], in_=phi[:, keys:HEADS, done, :])
+                masks(i, 0, keys)
+                nc.sync.dma_start(out=q_groups[b, c][:, :, done, :], in_=phi[:, 0:keys, done, :])
+                return
+            masks(i, 0, HEADS)
             if g >= TILES // GROUP - HALVED_GROUPS:
                 if t % PAIR == PAIR - 1:
                     done = slice(t - 1, t + 1)
-                    nc.sync.dma_start(out=q_groups[b, c][:, :, done, :], in_=phi[:, 0 : HEADS // 2, done, :])
-                    nc.sync.dma_start(out=k_groups[b, c][:, :, done, :], in_=phi[:, HEADS // 2 : HEADS, done, :])
+                    nc.sync.dma_start(out=q_groups[b, c][:, :, done, :], in_=phi[:, 0:keys, done, :])
+                    nc.sync.dma_start(out=k_groups[b, c][:, :, done, :], in_=phi[:, keys:HEADS, done, :])
             elif t == GROUP - 1:
-                nc.sync.dma_start(out=q_groups[b, c], in_=phi[:, 0 : HEADS // 2])
-                nc.sync.dma_start(out=k_groups[b, c], in_=phi[:, HEADS // 2 : HEADS])
+                nc.sync.dma_start(out=q_groups[b, c], in_=phi[:, 0:keys])
+                nc.sync.dma_start(out=k_groups[b, c], in_=phi[:, keys:HEADS])
 
         def due(step, lag, every=1):
             i = step - lag

@@ -35,7 +35,7 @@ LAG_SUMS = 6
 LAG_SCALE = 6
 LAG_MASK = 8
 POOL_HEADS = 1
-HALVED_GROUPS = 2
+HALVED_GROUPS = 4
 
 
 def tile_dpfpattention_pa_t_kernel(tc, x, w_qk_words, w_qk_scales, out_0, out_1):

from contextlib import ExitStack

import concourse.mybir as mybir
from concourse.masks import make_identity

F32 = mybir.dt.float32
BF16 = mybir.dt.bfloat16
I32 = mybir.dt.int32
U32 = mybir.dt.uint32
U8 = mybir.dt.uint8
FP8X4 = mybir.dt.float8_e4m3fn_x4
FP4X4 = mybir.dt.float4_e2m1fn_x4
ALU = mybir.AluOpType
ACT = mybir.ActivationFunctionType

P = 128
BATCH, TOKENS, K = 2, 2048, 512
HEADS, DH = 8, 64
COLS = HEADS * DH
GROUP = 4
GROUPS_PER_BATCH = TOKENS // (P * GROUP)
TILES = BATCH * TOKENS // P
PAIR = 2
WORDS = K // 2

FLOPS = 2 * BATCH * TOKENS * K * COLS

LAG_TRANSPOSE = 0
LAG_REGROUP = 1
LAG_QUANTISE = 2
LAG_PROJECT = 3
LAG_SHIFT = 4
LAG_PRODUCTS = 5
LAG_SUMS = 6
LAG_SCALE = 6
LAG_MASK = 8
POOL_HEADS = 1
HALVED_GROUPS = 4


def tile_dpfpattention_pa_t_kernel(tc, x, w_qk_words, w_qk_scales, out_0, out_1):
    nc = tc.nc
    x_groups = x.rearrange("b (c p t) k -> b c p t k", p=P, t=GROUP)
    q_groups = out_0.rearrange("b h (c p t) f -> b c p h t f", p=P, t=GROUP)
    k_groups = out_1.rearrange("b h (c p t) f -> b c p h t f", p=P, t=GROUP)

    with ExitStack() as ctx:
        const = ctx.enter_context(tc.tile_pool(name="const", bufs=1))
        x_pool = ctx.enter_context(tc.tile_pool(name="x_pool", bufs=TILES // GROUP))
        quant_pool = ctx.enter_context(tc.tile_pool(name="quant_pool", bufs=3))
        work = ctx.enter_context(tc.tile_pool(name="work", bufs=4))
        out_pool = ctx.enter_context(tc.tile_pool(name="out_pool", bufs=3))
        psum_t = ctx.enter_context(tc.psum_pool(name="psum_t", bufs=1))
        psum_u = ctx.enter_context(tc.psum_pool(name="psum_u", bufs=7))
        ctx.enter_context(tc.manual_schedule())

        x_tiles = []
        for g in range(TILES // GROUP):
            x_tiles.append(x_pool.tile([P, GROUP, K], BF16, name="x_sb"))

        def load_x(g):
            b, c = divmod(g, GROUPS_PER_BATCH)
            nc.sync.dma_start(out=x_tiles[g][:], in_=x_groups[b, c])

        w_plane = const.tile([P, COLS], U8, align_bytes=64)
        nc.vector.memset(w_plane[:].bitcast(I32), 0)
        w_words = const.tile([P, 2 * COLS], U8, align_bytes=64)

        nc.sync.dma_start(out=x_tiles[0][:, 0:1, :], in_=x_groups[0, 0][:, 0:1, :])
        nc.sync.dma_start(out=x_tiles[0][:, 1:PAIR, :], in_=x_groups[0, 0][:, 1:PAIR, :])
        nc.sync.dma_start(out=w_words[:].bitcast(I32), in_=w_qk_words[0].bitcast(I32))
        for quadrant in range(4):
            nc.sync.dma_start(
                out=w_plane[32 * quadrant : 32 * quadrant + 4, :].bitcast(I32),
                in_=w_qk_scales[0, 4 * quadrant : 4 * quadrant + 4, :].bitcast(I32),
            )
        nc.sync.dma_start(out=x_tiles[0][:, PAIR:GROUP, :], in_=x_groups[0, 0][:, PAIR:GROUP, :])
        for g in range(1, TILES // GROUP):
            load_x(g)

        identity = const.tile([P, P], F32)
        make_identity(nc, identity[:])

        xt_of, grouped_of, codes_of, scales_of = {}, {}, {}, {}
        u_of, prev_of, prod_of, relu_of, sums_of, scaled_of, phi_of = {}, {}, {}, {}, {}, {}, {}

        def transpose_pair(first):
            xt = psum_t.tile([P, PAIR, 2, P], F32, name="xt")
            xt_of[first] = xt
            for j in range(PAIR):
                g, t = divmod(first + j, GROUP)
                words = x_tiles[g][:].bitcast(F32)
                for half in range(2):
                    nc.tensor.transpose(xt[:, j, half, :], words[:, t, half:WORDS:2], identity[:])

        def regroup_pair(first):
            grouped = quant_pool.tile([P, PAIR, P, 4], BF16, name="grouped", align_bytes=64)
            grouped_of[first] = grouped
            if first == 0:
                for j in range(PAIR):
                    nc.scalar.copy(
                        out=grouped[:, j, :, :].bitcast(F32),
                        in_=xt_of[first][:, j, :, :].rearrange("p half r -> p r half"),
                    )
                return
            nc.scalar.copy(
                out=grouped[:].bitcast(F32),
                in_=xt_of[first][:].rearrange("p j half r -> p j r half"),
            )

        def quantise_pair(first):
            codes = quant_pool.tile([P, PAIR * P], U32, name="codes", align_bytes=64)
            scales = quant_pool.tile([P, PAIR * P], U8, name="scales", align_bytes=64)
            codes_of[first], scales_of[first] = codes, scales
            if first == 0:
                for j in range(PAIR):
                    tokens = slice(j * P, (j + 1) * P)
                    nc.vector.quantize_mx(
                        out=codes[:, tokens].bitcast(FP8X4),
                        scales=scales[:, tokens],
                        in_=grouped_of[first][:, j, :, :].rearrange("p r t -> p (r t)"),
                    )
                return
            nc.vector.quantize_mx(
                out=codes[:].bitcast(FP8X4),
                scales=scales[:],
                in_=grouped_of[first][:].rearrange("p j r t -> p (j r t)"),
            )

        def project(i):
            first, j = i - i % PAIR, i % PAIR
            tokens = slice(j * P, (j + 1) * P)
            u = psum_u.tile([P, HEADS, DH], F32, name="u")
            u_of[i] = u
            nc.tensor.matmul_mx(
                out=u[:].rearrange("p h d -> p (h d)"),
                lhsT=codes_of[first][:, tokens].bitcast(FP8X4),
                lhsT_scale=scales_of[first][:, tokens],
                rhs=w_words[:].bitcast(FP4X4),
                rhs_scale=w_plane[:],
                start=True,
                stop=True,
            )

        def shift(i):
            prev = work.tile([P, HEADS, DH], F32, name="prev")
            prev_of[i] = prev
            if i + LAG_SHIFT < LAG_MASK:
                nc.vector.tensor_copy(out=prev[:, :, 1:DH], in_=u_of[i][:, :, 0 : DH - 1])
                nc.vector.tensor_scalar_mul(
                    out=prev[:, :, 0:1], in0=u_of[i][:, :, DH - 1 : DH], scalar1=-1.0
                )
            else:
                nc.scalar.copy(out=prev[:, :, 1:DH], in_=u_of[i][:, :, 0 : DH - 1])
                nc.scalar.mul(out=prev[:, :, 0:1], in_=u_of[i][:, :, DH - 1 : DH], mul=-1.0)

        def products(i):
            prod = work.tile([P, HEADS, DH], F32, name="prod")
            prod_of[i] = prod
            nc.vector.tensor_tensor(out=prod[:], in0=u_of[i][:], in1=prev_of[i][:], op=ALU.mult)

        def sums(i):
            relu = work.tile([P, HEADS, DH], F32, name="relu")
            total = work.tile([P, HEADS], F32, name="total")
            relu_of[i], sums_of[i] = relu, total
            for h in range(HEADS):
                nc.scalar.activation(
                    out=relu[:, h, :],
                    in_=prod_of[i][:, h, :],
                    func=ACT.Relu,
                    accum_out=total[:, h : h + 1],
                )

        def scale(i):
            recip = work.tile([P, HEADS], F32, name="recip")
            nc.vector.reciprocal(recip[:], sums_of[i][:])
            scaled = work.tile([P, HEADS, DH], F32, name="scaled")
            scaled_of[i] = scaled
            nc.gpsimd.tensor_tensor(
                out=scaled[:],
                in0=relu_of[i][:],
                in1=recip[:].unsqueeze(2).to_broadcast([P, HEADS, DH]),
                op=ALU.mult,
            )

        def masks(i, lo, hi):
            g, t = divmod(i, GROUP)
            phi = phi_of[g]
            nc.vector.scalar_tensor_tensor(
                out=phi[:, lo:hi, t, 0:DH], in0=u_of[i][:, lo:hi, :], scalar=0.0,
                in1=scaled_of[i][:, lo:hi, :], op0=ALU.is_gt, op1=ALU.mult,
            )
            mine = min(hi, HEADS - POOL_HEADS)
            if mine < hi:
                nc.gpsimd.tensor_tensor(
                    out=phi[:, mine:hi, t, DH : 2 * DH], in0=scaled_of[i][:, mine:hi, :],
                    in1=phi[:, mine:hi, t, 0:DH], op=ALU.subtract,
                )
            nc.vector.scalar_tensor_tensor(
                out=phi[:, lo:mine, t, DH : 2 * DH], in0=u_of[i][:, lo:mine, :], scalar=0.0,
                in1=scaled_of[i][:, lo:mine, :], op0=ALU.is_lt, op1=ALU.mult,
            )

        def mask_and_store(i):
            g, t = divmod(i, GROUP)
            if t == 0:
                phi_of[g] = out_pool.tile([P, HEADS, GROUP, 2 * DH], F32, name="phi")
            phi = phi_of[g]
            b, c = divmod(g, GROUPS_PER_BATCH)
            keys = HEADS // 2
            if i == TILES - 1:
                done = slice(t - 1, t + 1)
                masks(i, keys, HEADS)
                nc.sync.dma_start(out=k_groups[b, c][:, :, done, :], in_=phi[:, keys:HEADS, done, :])
                masks(i, 0, keys)
                nc.sync.dma_start(out=q_groups[b, c][:, :, done, :], in_=phi[:, 0:keys, done, :])
                return
            masks(i, 0, HEADS)
            if g >= TILES // GROUP - HALVED_GROUPS:
                if t % PAIR == PAIR - 1:
                    done = slice(t - 1, t + 1)
                    nc.sync.dma_start(out=q_groups[b, c][:, :, done, :], in_=phi[:, 0:keys, done, :])
                    nc.sync.dma_start(out=k_groups[b, c][:, :, done, :], in_=phi[:, keys:HEADS, done, :])
            elif t == GROUP - 1:
                nc.sync.dma_start(out=q_groups[b, c], in_=phi[:, 0:keys])
                nc.sync.dma_start(out=k_groups[b, c], in_=phi[:, keys:HEADS])

        def due(step, lag, every=1):
            i = step - lag
            return 0 <= i < TILES and i % every == 0

        for step in range(TILES + LAG_MASK):
            if due(step, LAG_TRANSPOSE, PAIR):
                transpose_pair(step - LAG_TRANSPOSE)
            if due(step, LAG_PROJECT):
                project(step - LAG_PROJECT)
            if due(step, LAG_SHIFT):
                shift(step - LAG_SHIFT)
            if due(step, LAG_PRODUCTS):
                products(step - LAG_PRODUCTS)
            if due(step, LAG_REGROUP, PAIR):
                regroup_pair(step - LAG_REGROUP)
            if due(step, LAG_MASK):
                mask_and_store(step - LAG_MASK)
            if due(step, LAG_SUMS):
                sums(step - LAG_SUMS)
            if due(step, LAG_QUANTISE, PAIR):
                quantise_pair(step - LAG_QUANTISE)
            if due(step, LAG_SCALE):
                scale(step - LAG_SCALE)
